import numpy as np
import ml_dtypes


def mxq(x, axis, fmt="e4m3"):
    dtype, down = {"e4m3": (ml_dtypes.float8_e4m3fn, 7), "e5m2": (ml_dtypes.float8_e5m2, 14)}[fmt]
    v = np.moveaxis(np.asarray(x, np.float32).astype(ml_dtypes.bfloat16).astype(np.float64), axis, -1)
    blocks = v.reshape(v.shape[:-1] + (-1, 32))
    amax = np.abs(blocks).max(-1, keepdims=True)
    byte = np.maximum(np.where(amax > 0, np.frexp(amax)[1] - 1 + 127, 0) - down, 1)
    scale = np.exp2(byte - 127.0)
    codes = (blocks / scale).astype(np.float32).astype(dtype).astype(np.float64)
    return np.moveaxis((codes * scale).reshape(v.shape), -1, axis)


WIDE = False


def mx_kscale(k):
    if not WIDE:
        return np.ones(k)
    levels = np.array([10, -10, 5, -5, 0])
    if k % 512:
        return np.exp2(np.random.permutation(np.resize(levels, k // 32))).repeat(32)
    a = np.empty((k // 512, 16))
    for p in range(k // 512):
        a[p, :8] = np.random.permutation(np.resize(levels, 8))
        for g in range(8):
            far = levels[np.abs(levels - a[p, g]) >= 10]
            a[p, g + 8] = far[np.random.randint(len(far))]
    return np.exp2(a.ravel()).repeat(32)


BF16 = ml_dtypes.bfloat16


def bf(x):
    return np.asarray(x, np.float32).astype(BF16)


def f64(x):
    return np.asarray(x).astype(np.float64)


B, S, IQ, OQ, Q = 4, 1024, 512, 128, 4


def setup_inputs():
    s = mx_kscale(IQ)
    sw = 0.5 / np.sqrt(IQ)
    return {"x": bf((np.random.standard_normal((B, S, IQ, Q)) * s[:, None]).reshape(B, S, IQ * Q)),
            "wr": bf(np.random.standard_normal((OQ, IQ)) * sw / s),
            "wi": bf(np.random.standard_normal((OQ, IQ)) * sw / s),
            "wj": bf(np.random.standard_normal((OQ, IQ)) * sw / s),
            "wk": bf(np.random.standard_normal((OQ, IQ)) * sw / s),
            "bias": bf(np.random.standard_normal(OQ * Q) * 0.3)}


def reference(x, wr, wi, wj, wk, bias):
    xq = f64(x).reshape(B * S, IQ, Q)
    xr = mxq(xq[:, :, 0], 1, "e4m3")
    xi = mxq(xq[:, :, 1], 1, "e4m3")
    xj = mxq(xq[:, :, 2], 1, "e4m3")
    xk = mxq(xq[:, :, 3], 1, "e4m3")
    qr = mxq(f64(wr), 1, "e4m3")
    qi = mxq(f64(wi), 1, "e4m3")
    qj = mxq(f64(wj), 1, "e4m3")
    qk = mxq(f64(wk), 1, "e4m3")
    Ar = xr @ qr.T
    Br = xi @ qr.T
    Cr = xj @ qr.T
    Dr = xk @ qr.T
    Ai = xr @ qi.T
    Bi = xi @ qi.T
    Aj = xr @ qj.T
    Cj = xj @ qj.T
    Ak = xr @ qk.T
    Dk = xk @ qk.T
    or_ = Ar - Bi - Cj - Dk
    oi_ = Br + Ai + Dk - Cj
    oj_ = Cr - Dk + Aj + Bi
    ok_ = Dr + Cj - Bi + Ak
    out = np.stack([or_, oi_, oj_, ok_], axis=-1).reshape(B, S, Q * OQ)
    return out + f64(bias)[None, None, :]

@@ -1,0 +1,189 @@
+from contextlib import ExitStack
+
+import concourse.masks as masks
+import concourse.mybir as mybir
+
+BF16 = mybir.dt.bfloat16
+F32 = mybir.dt.float32
+U32 = mybir.dt.uint32
+U8 = mybir.dt.uint8
+FP8X4 = mybir.dt.float8_e4m3fn_x4
+
+P = 128
+PACK = 4
+HALVES = 2
+Q = 4
+IQ = 512
+OQ = 128
+ROWS = 4096
+TILES = 2
+N_CHUNKS = ROWS // (TILES * P)
+X_BUFS = 4
+AHEAD = 2
+SPLIT = 320
+
+FLOPS = 2 * ROWS * IQ * OQ * 10
+
+TERM = (
+    ((0, 1.0), (1, 1.0), (2, 1.0), (3, 1.0)),
+    ((1, -1.0), (0, 1.0), (1, 1.0), (1, -1.0)),
+    ((2, -1.0), (2, -1.0), (0, 1.0), (2, 1.0)),
+    ((3, -1.0), (3, 1.0), (3, -1.0), (0, 1.0)),
+)
+
+
+def tile_quaternionlinear_pa_t_kernel(tc, x, wr, wi, wj, wk, bias, out):
+    nc = tc.nc
+    x_rows = x.flatten_outer_dims()
+    out_rows = out.flatten_outer_dims()
+
+    with ExitStack() as stack:
+        const = stack.enter_context(tc.tile_pool(name="const", bufs=1))
+        x_pool = stack.enter_context(tc.tile_pool(name="x", bufs=X_BUFS))
+        sorted_pool = stack.enter_context(tc.tile_pool(name="sorted", bufs=AHEAD + 2))
+        grouped_pool = stack.enter_context(tc.tile_pool(name="grouped", bufs=2))
+        mx_pool = stack.enter_context(tc.tile_pool(name="mx", bufs=3))
+        out_pool = stack.enter_context(tc.tile_pool(name="out", bufs=3))
+        bank_pool = stack.enter_context(tc.psum_pool(name="bank", bufs=4))
+        acc_pool = stack.enter_context(tc.psum_pool(name="acc", bufs=4))
+        stack.enter_context(tc.manual_schedule())
+
+        x_raw = {}
+        x_sorted = {}
+        x_codes = {}
+        x_scales = {}
+        sums = {}
+
+        def tile_rows(dram, j, t):
+            first_row = (j * TILES + t) * P
+            return dram[first_row : first_row + P, :]
+
+        def load(j):
+            x_raw[j] = x_pool.tile([P, TILES, Q * IQ], BF16, name="x_raw")
+            for t in range(TILES):
+                nc.sync.dma_start(out=x_raw[j][:, t, :], in_=tile_rows(x_rows, j, t))
+
+        def sort_components(j):
+            x_sorted[j] = sorted_pool.tile([P, TILES, Q, IQ], BF16, name="x_sorted")
+            for t in range(TILES):
+                as_loaded = x_raw[j][:, t].rearrange("p (m u e c) -> p u m c e", u=2, e=2, c=Q)
+                by_component = x_sorted[j][:, t].rearrange("p c (u m e) -> p u m c e", u=2, e=2)
+                cut = SPLIT // PACK
+                nc.vector.tensor_copy(out=by_component[:, :, :cut], in_=as_loaded[:, :, :cut])
+                nc.scalar.copy(out=by_component[:, :, cut:], in_=as_loaded[:, :, cut:])
+            if j + X_BUFS < N_CHUNKS:
+                load(j + X_BUFS)
+
+        def k_on_partitions(words, grouped):
+            grouped_words = grouped.bitcast(F32)
+            for first in range(0, Q, 2):
+                bank = bank_pool.tile([P, 2, HALVES, P], F32, name="bank")
+                for c in range(2):
+                    for u in range(HALVES):
+                        nc.tensor.transpose(
+                            bank[:, c, u, :], words[:, first + c, u], ident[:]
+                        )
+                nc.scalar.copy(
+                    out=grouped_words[:, first : first + 2],
+                    in_=bank[:].rearrange("p c u r -> p c r u"),
+                )
+
+        def transpose(j):
+            x_grouped[j] = grouped_pool.tile(
+                [P, TILES, Q, P, PACK], BF16, name="x_grouped", align_bytes=64
+            )
+            for t in range(TILES):
+                k_on_partitions(
+                    x_sorted[j][:, t].bitcast(F32).rearrange("p c (u m) -> p c u m", u=HALVES),
+                    x_grouped[j][:, t],
+                )
+
+        def quantise(j):
+            x_codes[j] = mx_pool.tile([P, TILES, Q * P], U32, name="x_codes", align_bytes=64)
+            x_scales[j] = mx_pool.tile([P, TILES, Q * P], U8, name="x_scales", align_bytes=64)
+            for t in range(TILES):
+                nc.vector.quantize_mx(
+                    out=x_codes[j][:, t, :].bitcast(FP8X4),
+                    scales=x_scales[j][:, t, :],
+                    in_=x_grouped[j][:, t].rearrange("p c r k -> p (c r k)"),
+                )
+
+        def multiply(j):
+            for t in range(TILES):
+                sums[j, t] = acc_pool.tile([P, Q * OQ], F32, name="sums")
+                for a in range(Q):
+                    rows_of_a = slice(a * P, (a + 1) * P)
+                    nc.tensor.matmul_mx(
+                        out=sums[j, t][:],
+                        lhsT=x_codes[j][:, t, rows_of_a].bitcast(FP8X4),
+                        lhsT_scale=x_scales[j][:, t, rows_of_a],
+                        rhs=w_codes[:, a, :].bitcast(FP8X4),
+                        rhs_scale=w_scales[:, a, :],
+                        start=(a == 0),
+                        stop=(a == Q - 1),
+                    )
+
+        def finish(j):
+            result = out_pool.tile([P, TILES, Q * OQ], F32, name="result")
+            for t in range(TILES):
+                nc.vector.tensor_tensor(
+                    out=result[:, t, :].rearrange("p (o c) -> p o c", c=Q),
+                    in0=sums[j, t][:].rearrange("p (c o) -> p o c", c=Q),
+                    in1=bias_all[:].rearrange("p (o c) -> p o c", c=Q),
+                    op=mybir.AluOpType.add,
+                )
+                nc.sync.dma_start(out=tile_rows(out_rows, j, t), in_=result[:, t, :])
+
+        x_grouped = {}
+
+        w_rows = const.tile([P, Q, IQ], BF16)
+        for m, w in enumerate((wr, wi, wj, wk)):
+            nc.sync.dma_start(out=w_rows[:, m, :], in_=w)
+        bias_row = const.tile([P, Q * OQ], BF16)
+        nc.vector.memset(bias_row[:], 0.0)
+        nc.sync.dma_start(out=bias_row[0:1, :], in_=bias.unsqueeze(0))
+        for j in range(X_BUFS):
+            load(j)
+        ident = const.tile([P, P], F32)
+        masks.make_identity(nc, ident[:])
+        ones = const.tile([P, P], BF16)
+        nc.vector.memset(ones[:], 1.0)
+
+        w_grouped = const.tile([P, Q, Q, OQ, PACK], BF16, align_bytes=64)
+        w_codes = const.tile([P, Q, Q * OQ], U32, align_bytes=64)
+        w_scales = const.tile([P, Q, Q * OQ], U8, align_bytes=64)
+        k_on_partitions(
+            w_rows[:].bitcast(F32).rearrange("p c (m u) -> p c u m", u=HALVES), w_grouped[:, 0]
+        )
+
+        bias_spread = acc_pool.tile([P, Q * OQ], F32, name="sums")
+        nc.tensor.matmul(out=bias_spread[:], lhsT=ones[:], rhs=bias_row[:], start=True, stop=True)
+        bias_all = const.tile([P, Q * OQ], F32)
+        nc.scalar.copy(out=bias_all[:], in_=bias_spread[:])
+
+        sort_components(0)
+        for a in range(1, Q):
+            for c in range(Q):
+                m, sign = TERM[a][c]
+                nc.vector.tensor_scalar_mul(
+                    out=w_grouped[:, a, c], in0=w_grouped[:, 0, m], scalar1=sign
+                )
+        for a in range(Q):
+            nc.vector.quantize_mx(
+                out=w_codes[:, a, :].bitcast(FP8X4),
+                scales=w_scales[:, a, :],
+                in_=w_grouped[:, a].rearrange("p c o t -> p (c o t)"),
+            )
+        sort_components(1)
+
+        for j in range(N_CHUNKS + 1):
+            if j < N_CHUNKS:
+                transpose(j)
+            if j >= 1:
+                multiply(j - 1)
+            if j < N_CHUNKS:
+                quantise(j)
+            if j >= 1:
+                finish(j - 1)
+            if j + AHEAD < N_CHUNKS:
+                sort_components(j + AHEAD)

@@ -20,7 +20,7 @@ TILES = 2
 N_CHUNKS = ROWS // (TILES * P)
 X_BUFS = 4
 AHEAD = 2
-SPLIT = 320
+SPLIT = 336
 
 FLOPS = 2 * ROWS * IQ * OQ * 10
 
@@ -30,6 +30,18 @@ TERM = (
     ((2, -1.0), (2, -1.0), (0, 1.0), (2, 1.0)),
     ((3, -1.0), (3, 1.0), (3, -1.0), (0, 1.0)),
 )
+
+PLANES = (
+    (3, -1.0), (0, 1.0), (1, 1.0), (1, -1.0), (0, 1.0), (2, 1.0), (3, 1.0),
+    (3, -1.0), (3, 1.0),
+    (2, -1.0), (2, -1.0),
+)
+PAIR = 2
+
+
+def first_plane(a, h):
+    pair = TERM[a][PAIR * h : PAIR * h + PAIR]
+    return [PLANES[s : s + PAIR] for s in range(len(PLANES))].index(pair)
 
 
 def tile_quaternionlinear_pa_t_kernel(tc, x, wr, wi, wj, wk, bias, out):
@@ -74,18 +86,16 @@ def tile_quaternionlinear_pa_t_kernel(tc, x, wr, wi, wj, wk, bias, out):
             if j + X_BUFS < N_CHUNKS:
                 load(j + X_BUFS)
 
-        def k_on_partitions(words, grouped):
-            grouped_words = grouped.bitcast(F32)
-            for first in range(0, Q, 2):
+        def k_on_partitions(words, grouped_pairs):
+            for pair, grouped in enumerate(grouped_pairs):
                 bank = bank_pool.tile([P, 2, HALVES, P], F32, name="bank")
                 for c in range(2):
                     for u in range(HALVES):
                         nc.tensor.transpose(
-                            bank[:, c, u, :], words[:, first + c, u], ident[:]
+                            bank[:, c, u, :], words[:, PAIR * pair + c, u], ident[:]
                         )
                 nc.scalar.copy(
-                    out=grouped_words[:, first : first + 2],
-                    in_=bank[:].rearrange("p c u r -> p c r u"),
+                    out=grouped.bitcast(F32), in_=bank[:].rearrange("p c u r -> p c r u")
                 )
 
         def transpose(j):
@@ -95,7 +105,7 @@ def tile_quaternionlinear_pa_t_kernel(tc, x, wr, wi, wj, wk, bias, out):
             for t in range(TILES):
                 k_on_partitions(
                     x_sorted[j][:, t].bitcast(F32).rearrange("p c (u m) -> p c u m", u=HALVES),
-                    x_grouped[j][:, t],
+                    (x_grouped[j][:, t, :PAIR], x_grouped[j][:, t, PAIR:]),
                 )
 
         def quantise(j):
@@ -111,17 +121,19 @@ def tile_quaternionlinear_pa_t_kernel(tc, x, wr, wi, wj, wk, bias, out):
         def multiply(j):
             for t in range(TILES):
                 sums[j, t] = acc_pool.tile([P, Q * OQ], F32, name="sums")
-                for a in range(Q):
-                    rows_of_a = slice(a * P, (a + 1) * P)
-                    nc.tensor.matmul_mx(
-                        out=sums[j, t][:],
-                        lhsT=x_codes[j][:, t, rows_of_a].bitcast(FP8X4),
-                        lhsT_scale=x_scales[j][:, t, rows_of_a],
-                        rhs=w_codes[:, a, :].bitcast(FP8X4),
-                        rhs_scale=w_scales[:, a, :],
-                        start=(a == 0),
-                        stop=(a == Q - 1),
-                    )
+                for h in range(Q // PAIR):
+                    for a in range(Q):
+                        rows_of_a = slice(a * P, (a + 1) * P)
+                        s = first_plane(a, h)
+                        nc.tensor.matmul_mx(
+                            out=sums[j, t][:, h * PAIR * OQ : (h + 1) * PAIR * OQ],
+                            lhsT=x_codes[j][:, t, rows_of_a].bitcast(FP8X4),
+                            lhsT_scale=x_scales[j][:, t, rows_of_a],
+                            rhs=w_codes[:, s * OQ : (s + PAIR) * OQ].bitcast(FP8X4),
+                            rhs_scale=w_scales[:, s * OQ : (s + PAIR) * OQ],
+                            start=(a == 0),
+                            stop=(a == Q - 1),
+                        )
 
         def finish(j):
             result = out_pool.tile([P, TILES, Q * OQ], F32, name="result")
@@ -149,11 +161,13 @@ def tile_quaternionlinear_pa_t_kernel(tc, x, wr, wi, wj, wk, bias, out):
         ones = const.tile([P, P], BF16)
         nc.vector.memset(ones[:], 1.0)
 
-        w_grouped = const.tile([P, Q, Q, OQ, PACK], BF16, align_bytes=64)
-        w_codes = const.tile([P, Q, Q * OQ], U32, align_bytes=64)
-        w_scales = const.tile([P, Q, Q * OQ], U8, align_bytes=64)
+        w_grouped = const.tile([P, len(PLANES), OQ, PACK], BF16, align_bytes=64)
+        w_codes = const.tile([P, len(PLANES) * OQ], U32, align_bytes=64)
+        w_scales = const.tile([P, len(PLANES) * OQ], U8, align_bytes=64)
+        as_they_are = [first_plane(0, h) for h in range(Q // PAIR)]
         k_on_partitions(
-            w_rows[:].bitcast(F32).rearrange("p c (m u) -> p c u m", u=HALVES), w_grouped[:, 0]
+            w_rows[:].bitcast(F32).rearrange("p c (m u) -> p c u m", u=HALVES),
+            [w_grouped[:, s : s + PAIR] for s in as_they_are],
         )
 
         bias_spread = acc_pool.tile([P, Q * OQ], F32, name="sums")
@@ -162,17 +176,18 @@ def tile_quaternionlinear_pa_t_kernel(tc, x, wr, wi, wj, wk, bias, out):
         nc.scalar.copy(out=bias_all[:], in_=bias_spread[:])
 
         sort_components(0)
-        for a in range(1, Q):
-            for c in range(Q):
-                m, sign = TERM[a][c]
+        source = {PAIR * h + n: s + n for h, s in enumerate(as_they_are) for n in range(PAIR)}
+        for s, (m, sign) in enumerate(PLANES):
+            if s not in source.values():
                 nc.vector.tensor_scalar_mul(
-                    out=w_grouped[:, a, c], in0=w_grouped[:, 0, m], scalar1=sign
+                    out=w_grouped[:, s], in0=w_grouped[:, source[m]], scalar1=sign
                 )
-        for a in range(Q):
+        for first, last in ((0, 4), (4, 8), (8, 10), (10, 11)):
+            columns = slice(first * OQ, last * OQ)
             nc.vector.quantize_mx(
-                out=w_codes[:, a, :].bitcast(FP8X4),
-                scales=w_scales[:, a, :],
-                in_=w_grouped[:, a].rearrange("p c o t -> p (c o t)"),
+                out=w_codes[:, columns].bitcast(FP8X4),
+                scales=w_scales[:, columns],
+                in_=w_grouped[:, first:last].rearrange("p s o t -> p (s o t)"),
             )
         sort_components(1)
 

@@ -6,6 +6,7 @@ import concourse.mybir as mybir
 BF16 = mybir.dt.bfloat16
 F32 = mybir.dt.float32
 U32 = mybir.dt.uint32
+I32 = mybir.dt.int32
 U8 = mybir.dt.uint8
 FP8X4 = mybir.dt.float8_e4m3fn_x4
 
@@ -31,17 +32,10 @@ TERM = (
     ((3, -1.0), (3, 1.0), (3, -1.0), (0, 1.0)),
 )
 
-PLANES = (
-    (3, -1.0), (0, 1.0), (1, 1.0), (1, -1.0), (0, 1.0), (2, 1.0), (3, 1.0),
-    (3, -1.0), (3, 1.0),
-    (2, -1.0), (2, -1.0),
-)
+PLANES = ((0, 1.0), (1, 1.0), (2, 1.0), (3, 1.0), (1, -1.0), (2, -1.0), (3, -1.0))
+OPERANDS = [term for terms in TERM for term in terms]
+QUANTISED = ((0, 4, 0), (4, 2, 7), (6, 1, 12))
 PAIR = 2
-
-
-def first_plane(a, h):
-    pair = TERM[a][PAIR * h : PAIR * h + PAIR]
-    return [PLANES[s : s + PAIR] for s in range(len(PLANES))].index(pair)
 
 
 def tile_quaternionlinear_pa_t_kernel(tc, x, wr, wi, wj, wk, bias, out):
@@ -65,6 +59,7 @@ def tile_quaternionlinear_pa_t_kernel(tc, x, wr, wi, wj, wk, bias, out):
         x_codes = {}
         x_scales = {}
         sums = {}
+        results = {}
 
         def tile_rows(dram, j, t):
             first_row = (j * TILES + t) * P
@@ -108,43 +103,41 @@ def tile_quaternionlinear_pa_t_kernel(tc, x, wr, wi, wj, wk, bias, out):
                     (x_grouped[j][:, t, :PAIR], x_grouped[j][:, t, PAIR:]),
                 )
 
-        def quantise(j):
-            x_codes[j] = mx_pool.tile([P, TILES, Q * P], U32, name="x_codes", align_bytes=64)
-            x_scales[j] = mx_pool.tile([P, TILES, Q * P], U8, name="x_scales", align_bytes=64)
-            for t in range(TILES):
-                nc.vector.quantize_mx(
-                    out=x_codes[j][:, t, :].bitcast(FP8X4),
-                    scales=x_scales[j][:, t, :],
-                    in_=x_grouped[j][:, t].rearrange("p c r k -> p (c r k)"),
-                )
+        def quantise(j, t):
+            if t == 0:
+                x_codes[j] = mx_pool.tile([P, TILES, Q * P], U32, name="x_codes", align_bytes=64)
+                x_scales[j] = mx_pool.tile([P, TILES, Q * P], U8, name="x_scales", align_bytes=64)
+            nc.vector.quantize_mx(
+                out=x_codes[j][:, t, :].bitcast(FP8X4),
+                scales=x_scales[j][:, t, :],
+                in_=x_grouped[j][:, t].rearrange("p c r k -> p (c r k)"),
+            )
 
         def multiply(j):
             for t in range(TILES):
                 sums[j, t] = acc_pool.tile([P, Q * OQ], F32, name="sums")
-                for h in range(Q // PAIR):
-                    for a in range(Q):
-                        rows_of_a = slice(a * P, (a + 1) * P)
-                        s = first_plane(a, h)
-                        nc.tensor.matmul_mx(
-                            out=sums[j, t][:, h * PAIR * OQ : (h + 1) * PAIR * OQ],
-                            lhsT=x_codes[j][:, t, rows_of_a].bitcast(FP8X4),
-                            lhsT_scale=x_scales[j][:, t, rows_of_a],
-                            rhs=w_codes[:, s * OQ : (s + PAIR) * OQ].bitcast(FP8X4),
-                            rhs_scale=w_scales[:, s * OQ : (s + PAIR) * OQ],
-                            start=(a == 0),
-                            stop=(a == Q - 1),
-                        )
+                for a in range(Q):
+                    rows_of_a = slice(a * P, (a + 1) * P)
+                    nc.tensor.matmul_mx(
+                        out=sums[j, t][:],
+                        lhsT=x_codes[j][:, t, rows_of_a].bitcast(FP8X4),
+                        lhsT_scale=x_scales[j][:, t, rows_of_a],
+                        rhs=w_codes[:, a * Q * OQ : (a + 1) * Q * OQ].bitcast(FP8X4),
+                        rhs_scale=w_scales[:, a * Q * OQ : (a + 1) * Q * OQ],
+                        start=(a == 0),
+                        stop=(a == Q - 1),
+                    )
 
-        def finish(j):
-            result = out_pool.tile([P, TILES, Q * OQ], F32, name="result")
-            for t in range(TILES):
-                nc.vector.tensor_tensor(
-                    out=result[:, t, :].rearrange("p (o c) -> p o c", c=Q),
-                    in0=sums[j, t][:].rearrange("p (c o) -> p o c", c=Q),
-                    in1=bias_all[:].rearrange("p (o c) -> p o c", c=Q),
-                    op=mybir.AluOpType.add,
-                )
-                nc.sync.dma_start(out=tile_rows(out_rows, j, t), in_=result[:, t, :])
+        def finish(j, t):
+            if t == 0:
+                results[j] = out_pool.tile([P, TILES, Q * OQ], F32, name="result")
+            nc.vector.tensor_tensor(
+                out=results[j][:, t, :].rearrange("p (o c) -> p o c", c=Q),
+                in0=sums[j, t][:].rearrange("p (c o) -> p o c", c=Q),
+                in1=bias_all[:].rearrange("p (o c) -> p o c", c=Q),
+                op=mybir.AluOpType.add,
+            )
+            nc.sync.dma_start(out=tile_rows(out_rows, j, t), in_=results[j][:, t, :])
 
         x_grouped = {}
 
@@ -162,12 +155,11 @@ def tile_quaternionlinear_pa_t_kernel(tc, x, wr, wi, wj, wk, bias, out):
         nc.vector.memset(ones[:], 1.0)
 
         w_grouped = const.tile([P, len(PLANES), OQ, PACK], BF16, align_bytes=64)
-        w_codes = const.tile([P, len(PLANES) * OQ], U32, align_bytes=64)
-        w_scales = const.tile([P, len(PLANES) * OQ], U8, align_bytes=64)
-        as_they_are = [first_plane(0, h) for h in range(Q // PAIR)]
+        w_codes = const.tile([P, len(OPERANDS) * OQ], U32, align_bytes=64)
+        w_scales = const.tile([P, len(OPERANDS) * OQ], U8, align_bytes=64)
         k_on_partitions(
             w_rows[:].bitcast(F32).rearrange("p c (m u) -> p c u m", u=HALVES),
-            [w_grouped[:, s : s + PAIR] for s in as_they_are],
+            (w_grouped[:, 0:PAIR], w_grouped[:, PAIR:Q]),
         )
 
         bias_spread = acc_pool.tile([P, Q * OQ], F32, name="sums")
@@ -176,19 +168,31 @@ def tile_quaternionlinear_pa_t_kernel(tc, x, wr, wi, wj, wk, bias, out):
         nc.scalar.copy(out=bias_all[:], in_=bias_spread[:])
 
         sort_components(0)
-        source = {PAIR * h + n: s + n for h, s in enumerate(as_they_are) for n in range(PAIR)}
-        for s, (m, sign) in enumerate(PLANES):
-            if s not in source.values():
-                nc.vector.tensor_scalar_mul(
-                    out=w_grouped[:, s], in0=w_grouped[:, source[m]], scalar1=sign
-                )
-        for first, last in ((0, 4), (4, 8), (8, 10), (10, 11)):
-            columns = slice(first * OQ, last * OQ)
+        for s, (m, sign) in enumerate(PLANES[Q:]):
+            nc.vector.tensor_scalar_mul(
+                out=w_grouped[:, Q + s], in0=w_grouped[:, m], scalar1=sign
+            )
+        place_of = {}
+        for plane, planes, place in QUANTISED:
+            columns = slice(place * OQ, (place + planes) * OQ)
             nc.vector.quantize_mx(
                 out=w_codes[:, columns].bitcast(FP8X4),
                 scales=w_scales[:, columns],
-                in_=w_grouped[:, first:last].rearrange("p s o t -> p (s o t)"),
+                in_=w_grouped[:, plane : plane + planes].rearrange("p s o t -> p (s o t)"),
             )
+            for n in range(planes):
+                place_of[PLANES[plane + n]] = place + n
+        codes = w_codes[:].bitcast(I32)
+        scales = w_scales[:].bitcast(I32)
+        for place, term in enumerate(OPERANDS):
+            if place not in place_of.values():
+                for whole in (codes, scales):
+                    words = whole.shape[1] // len(OPERANDS)
+                    source = place_of[term]
+                    nc.vector.tensor_copy(
+                        out=whole[:, place * words : (place + 1) * words],
+                        in_=whole[:, source * words : (source + 1) * words],
+                    )
         sort_components(1)
 
         for j in range(N_CHUNKS + 1):
@@ -196,9 +200,10 @@ def tile_quaternionlinear_pa_t_kernel(tc, x, wr, wi, wj, wk, bias, out):
                 transpose(j)
             if j >= 1:
                 multiply(j - 1)
-            if j < N_CHUNKS:
-                quantise(j)
-            if j >= 1:
-                finish(j - 1)
+            for t in range(TILES):
+                if j < N_CHUNKS:
+                    quantise(j, t)
+                if j >= 1:
+                    finish(j - 1, t)
             if j + AHEAD < N_CHUNKS:
                 sort_components(j + AHEAD)

@@ -21,7 +21,7 @@ TILES = 2
 N_CHUNKS = ROWS // (TILES * P)
 X_BUFS = 4
 AHEAD = 2
-SPLIT = 336
+SPLIT = 344
 
 FLOPS = 2 * ROWS * IQ * OQ * 10
 
@@ -162,12 +162,13 @@ def tile_quaternionlinear_pa_t_kernel(tc, x, wr, wi, wj, wk, bias, out):
             (w_grouped[:, 0:PAIR], w_grouped[:, PAIR:Q]),
         )
 
+        sort_components(0)
+
         bias_spread = acc_pool.tile([P, Q * OQ], F32, name="sums")
         nc.tensor.matmul(out=bias_spread[:], lhsT=ones[:], rhs=bias_row[:], start=True, stop=True)
         bias_all = const.tile([P, Q * OQ], F32)
         nc.scalar.copy(out=bias_all[:], in_=bias_spread[:])
 
-        sort_components(0)
         for s, (m, sign) in enumerate(PLANES[Q:]):
             nc.vector.tensor_scalar_mul(
                 out=w_grouped[:, Q + s], in0=w_grouped[:, m], scalar1=sign

@@ -21,6 +21,7 @@ TILES = 2
 N_CHUNKS = ROWS // (TILES * P)
 X_BUFS = 4
 AHEAD = 2
+UNSORTED = AHEAD
 SPLIT = 344
 
 FLOPS = 2 * ROWS * IQ * OQ * 10
@@ -103,6 +104,23 @@ def tile_quaternionlinear_pa_t_kernel(tc, x, wr, wi, wj, wk, bias, out):
                     (x_grouped[j][:, t, :PAIR], x_grouped[j][:, t, PAIR:]),
                 )
 
+        def transpose_unsorted(j):
+            x_grouped[j] = grouped_pool.tile(
+                [P, TILES, Q, P, PACK], BF16, name="x_grouped", align_bytes=64
+            )
+            for t in range(TILES):
+                words = x_raw[j][:, t, :].bitcast(F32)
+                for h in range(Q // 2):
+                    bank = bank_pool.tile([P, PACK, P], F32, name="bank")
+                    for k in range(PACK):
+                        nc.tensor.transpose(bank[:, k, :], words[:, 2 * k + h :: 2 * PACK], ident[:])
+                    copy = nc.vector.tensor_copy if (t, h) == (1, 1) else nc.scalar.copy
+                    copy(
+                        out=x_grouped[j][:, t, 2 * h : 2 * h + 2],
+                        in_=bank[:].bitcast(BF16).rearrange("p k (r e) -> p e r k", e=2),
+                    )
+            load(j + X_BUFS)
+
         def quantise(j, t):
             if t == 0:
                 x_codes[j] = mx_pool.tile([P, TILES, Q * P], U32, name="x_codes", align_bytes=64)
@@ -162,8 +180,6 @@ def tile_quaternionlinear_pa_t_kernel(tc, x, wr, wi, wj, wk, bias, out):
             (w_grouped[:, 0:PAIR], w_grouped[:, PAIR:Q]),
         )
 
-        sort_components(0)
-
         bias_spread = acc_pool.tile([P, Q * OQ], F32, name="sums")
         nc.tensor.matmul(out=bias_spread[:], lhsT=ones[:], rhs=bias_row[:], start=True, stop=True)
         bias_all = const.tile([P, Q * OQ], F32)
@@ -194,17 +210,27 @@ def tile_quaternionlinear_pa_t_kernel(tc, x, wr, wi, wj, wk, bias, out):
                         out=whole[:, place * words : (place + 1) * words],
                         in_=whole[:, source * words : (source + 1) * words],
                     )
-        sort_components(1)
+        for j in range(UNSORTED):
+            transpose_unsorted(j)
+            if j >= 1:
+                multiply(j - 1)
+            for t in range(TILES):
+                quantise(j, t)
+        multiply(UNSORTED - 1)
+        for j in range(UNSORTED, UNSORTED + AHEAD):
+            sort_components(j)
+        for j in range(UNSORTED - 1):
+            for t in range(TILES):
+                finish(j, t)
 
-        for j in range(N_CHUNKS + 1):
+        for j in range(UNSORTED, N_CHUNKS + 1):
             if j < N_CHUNKS:
                 transpose(j)
-            if j >= 1:
+            if j > UNSORTED:
                 multiply(j - 1)
             for t in range(TILES):
                 if j < N_CHUNKS:
                     quantise(j, t)
-                if j >= 1:
-                    finish(j - 1, t)
+                finish(j - 1, t)
             if j + AHEAD < N_CHUNKS:
                 sort_components(j + AHEAD)

from contextlib import ExitStack

import concourse.masks as masks
import concourse.mybir as mybir

BF16 = mybir.dt.bfloat16
F32 = mybir.dt.float32
U32 = mybir.dt.uint32
I32 = mybir.dt.int32
U8 = mybir.dt.uint8
FP8X4 = mybir.dt.float8_e4m3fn_x4

P = 128
PACK = 4
HALVES = 2
Q = 4
IQ = 512
OQ = 128
ROWS = 4096
TILES = 2
N_CHUNKS = ROWS // (TILES * P)
X_BUFS = 4
AHEAD = 2
UNSORTED = AHEAD
SPLIT = 344

FLOPS = 2 * ROWS * IQ * OQ * 10

TERM = (
    ((0, 1.0), (1, 1.0), (2, 1.0), (3, 1.0)),
    ((1, -1.0), (0, 1.0), (1, 1.0), (1, -1.0)),
    ((2, -1.0), (2, -1.0), (0, 1.0), (2, 1.0)),
    ((3, -1.0), (3, 1.0), (3, -1.0), (0, 1.0)),
)

PLANES = ((0, 1.0), (1, 1.0), (2, 1.0), (3, 1.0), (1, -1.0), (2, -1.0), (3, -1.0))
OPERANDS = [term for terms in TERM for term in terms]
QUANTISED = ((0, 4, 0), (4, 2, 7), (6, 1, 12))
PAIR = 2


def tile_quaternionlinear_pa_t_kernel(tc, x, wr, wi, wj, wk, bias, out):
    nc = tc.nc
    x_rows = x.flatten_outer_dims()
    out_rows = out.flatten_outer_dims()

    with ExitStack() as stack:
        const = stack.enter_context(tc.tile_pool(name="const", bufs=1))
        x_pool = stack.enter_context(tc.tile_pool(name="x", bufs=X_BUFS))
        sorted_pool = stack.enter_context(tc.tile_pool(name="sorted", bufs=AHEAD + 2))
        grouped_pool = stack.enter_context(tc.tile_pool(name="grouped", bufs=2))
        mx_pool = stack.enter_context(tc.tile_pool(name="mx", bufs=3))
        out_pool = stack.enter_context(tc.tile_pool(name="out", bufs=3))
        bank_pool = stack.enter_context(tc.psum_pool(name="bank", bufs=4))
        acc_pool = stack.enter_context(tc.psum_pool(name="acc", bufs=4))
        stack.enter_context(tc.manual_schedule())

        x_raw = {}
        x_sorted = {}
        x_codes = {}
        x_scales = {}
        sums = {}
        results = {}

        def tile_rows(dram, j, t):
            first_row = (j * TILES + t) * P
            return dram[first_row : first_row + P, :]

        def load(j):
            x_raw[j] = x_pool.tile([P, TILES, Q * IQ], BF16, name="x_raw")
            for t in range(TILES):
                nc.sync.dma_start(out=x_raw[j][:, t, :], in_=tile_rows(x_rows, j, t))

        def sort_components(j):
            x_sorted[j] = sorted_pool.tile([P, TILES, Q, IQ], BF16, name="x_sorted")
            for t in range(TILES):
                as_loaded = x_raw[j][:, t].rearrange("p (m u e c) -> p u m c e", u=2, e=2, c=Q)
                by_component = x_sorted[j][:, t].rearrange("p c (u m e) -> p u m c e", u=2, e=2)
                cut = SPLIT // PACK
                nc.vector.tensor_copy(out=by_component[:, :, :cut], in_=as_loaded[:, :, :cut])
                nc.scalar.copy(out=by_component[:, :, cut:], in_=as_loaded[:, :, cut:])
            if j + X_BUFS < N_CHUNKS:
                load(j + X_BUFS)

        def k_on_partitions(words, grouped_pairs):
            for pair, grouped in enumerate(grouped_pairs):
                bank = bank_pool.tile([P, 2, HALVES, P], F32, name="bank")
                for c in range(2):
                    for u in range(HALVES):
                        nc.tensor.transpose(
                            bank[:, c, u, :], words[:, PAIR * pair + c, u], ident[:]
                        )
                nc.scalar.copy(
                    out=grouped.bitcast(F32), in_=bank[:].rearrange("p c u r -> p c r u")
                )

        def transpose(j):
            x_grouped[j] = grouped_pool.tile(
                [P, TILES, Q, P, PACK], BF16, name="x_grouped", align_bytes=64
            )
            for t in range(TILES):
                k_on_partitions(
                    x_sorted[j][:, t].bitcast(F32).rearrange("p c (u m) -> p c u m", u=HALVES),
                    (x_grouped[j][:, t, :PAIR], x_grouped[j][:, t, PAIR:]),
                )

        def transpose_unsorted(j):
            x_grouped[j] = grouped_pool.tile(
                [P, TILES, Q, P, PACK], BF16, name="x_grouped", align_bytes=64
            )
            for t in range(TILES):
                words = x_raw[j][:, t, :].bitcast(F32)
                for h in range(Q // 2):
                    bank = bank_pool.tile([P, PACK, P], F32, name="bank")
                    for k in range(PACK):
                        nc.tensor.transpose(bank[:, k, :], words[:, 2 * k + h :: 2 * PACK], ident[:])
                    copy = nc.vector.tensor_copy if (t, h) == (1, 1) else nc.scalar.copy
                    copy(
                        out=x_grouped[j][:, t, 2 * h : 2 * h + 2],
                        in_=bank[:].bitcast(BF16).rearrange("p k (r e) -> p e r k", e=2),
                    )
            load(j + X_BUFS)

        def quantise(j, t):
            if t == 0:
                x_codes[j] = mx_pool.tile([P, TILES, Q * P], U32, name="x_codes", align_bytes=64)
                x_scales[j] = mx_pool.tile([P, TILES, Q * P], U8, name="x_scales", align_bytes=64)
            nc.vector.quantize_mx(
                out=x_codes[j][:, t, :].bitcast(FP8X4),
                scales=x_scales[j][:, t, :],
                in_=x_grouped[j][:, t].rearrange("p c r k -> p (c r k)"),
            )

        def multiply(j):
            for t in range(TILES):
                sums[j, t] = acc_pool.tile([P, Q * OQ], F32, name="sums")
                for a in range(Q):
                    rows_of_a = slice(a * P, (a + 1) * P)
                    nc.tensor.matmul_mx(
                        out=sums[j, t][:],
                        lhsT=x_codes[j][:, t, rows_of_a].bitcast(FP8X4),
                        lhsT_scale=x_scales[j][:, t, rows_of_a],
                        rhs=w_codes[:, a * Q * OQ : (a + 1) * Q * OQ].bitcast(FP8X4),
                        rhs_scale=w_scales[:, a * Q * OQ : (a + 1) * Q * OQ],
                        start=(a == 0),
                        stop=(a == Q - 1),
                    )

        def finish(j, t):
            if t == 0:
                results[j] = out_pool.tile([P, TILES, Q * OQ], F32, name="result")
            nc.vector.tensor_tensor(
                out=results[j][:, t, :].rearrange("p (o c) -> p o c", c=Q),
                in0=sums[j, t][:].rearrange("p (c o) -> p o c", c=Q),
                in1=bias_all[:].rearrange("p (o c) -> p o c", c=Q),
                op=mybir.AluOpType.add,
            )
            nc.sync.dma_start(out=tile_rows(out_rows, j, t), in_=results[j][:, t, :])

        x_grouped = {}

        w_rows = const.tile([P, Q, IQ], BF16)
        for m, w in enumerate((wr, wi, wj, wk)):
            nc.sync.dma_start(out=w_rows[:, m, :], in_=w)
        bias_row = const.tile([P, Q * OQ], BF16)
        nc.vector.memset(bias_row[:], 0.0)
        nc.sync.dma_start(out=bias_row[0:1, :], in_=bias.unsqueeze(0))
        for j in range(X_BUFS):
            load(j)
        ident = const.tile([P, P], F32)
        masks.make_identity(nc, ident[:])
        ones = const.tile([P, P], BF16)
        nc.vector.memset(ones[:], 1.0)

        w_grouped = const.tile([P, len(PLANES), OQ, PACK], BF16, align_bytes=64)
        w_codes = const.tile([P, len(OPERANDS) * OQ], U32, align_bytes=64)
        w_scales = const.tile([P, len(OPERANDS) * OQ], U8, align_bytes=64)
        k_on_partitions(
            w_rows[:].bitcast(F32).rearrange("p c (m u) -> p c u m", u=HALVES),
            (w_grouped[:, 0:PAIR], w_grouped[:, PAIR:Q]),
        )

        bias_spread = acc_pool.tile([P, Q * OQ], F32, name="sums")
        nc.tensor.matmul(out=bias_spread[:], lhsT=ones[:], rhs=bias_row[:], start=True, stop=True)
        bias_all = const.tile([P, Q * OQ], F32)
        nc.scalar.copy(out=bias_all[:], in_=bias_spread[:])

        for s, (m, sign) in enumerate(PLANES[Q:]):
            nc.vector.tensor_scalar_mul(
                out=w_grouped[:, Q + s], in0=w_grouped[:, m], scalar1=sign
            )
        place_of = {}
        for plane, planes, place in QUANTISED:
            columns = slice(place * OQ, (place + planes) * OQ)
            nc.vector.quantize_mx(
                out=w_codes[:, columns].bitcast(FP8X4),
                scales=w_scales[:, columns],
                in_=w_grouped[:, plane : plane + planes].rearrange("p s o t -> p (s o t)"),
            )
            for n in range(planes):
                place_of[PLANES[plane + n]] = place + n
        codes = w_codes[:].bitcast(I32)
        scales = w_scales[:].bitcast(I32)
        for place, term in enumerate(OPERANDS):
            if place not in place_of.values():
                for whole in (codes, scales):
                    words = whole.shape[1] // len(OPERANDS)
                    source = place_of[term]
                    nc.vector.tensor_copy(
                        out=whole[:, place * words : (place + 1) * words],
                        in_=whole[:, source * words : (source + 1) * words],
                    )
        for j in range(UNSORTED):
            transpose_unsorted(j)
            if j >= 1:
                multiply(j - 1)
            for t in range(TILES):
                quantise(j, t)
        multiply(UNSORTED - 1)
        for j in range(UNSORTED, UNSORTED + AHEAD):
            sort_components(j)
        for j in range(UNSORTED - 1):
            for t in range(TILES):
                finish(j, t)

        for j in range(UNSORTED, N_CHUNKS + 1):
            if j < N_CHUNKS:
                transpose(j)
            if j > UNSORTED:
                multiply(j - 1)
            for t in range(TILES):
                if j < N_CHUNKS:
                    quantise(j, t)
                finish(j - 1, t)
            if j + AHEAD < N_CHUNKS:
                sort_components(j + AHEAD)
